import numpy as np
import ml_dtypes


def mxq(x, axis, fmt="e4m3"):
    dtype, down = {"e4m3": (ml_dtypes.float8_e4m3fn, 7), "e5m2": (ml_dtypes.float8_e5m2, 14)}[fmt]
    v = np.moveaxis(np.asarray(x, np.float32).astype(ml_dtypes.bfloat16).astype(np.float64), axis, -1)
    blocks = v.reshape(v.shape[:-1] + (-1, 32))
    amax = np.abs(blocks).max(-1, keepdims=True)
    byte = np.maximum(np.where(amax > 0, np.frexp(amax)[1] - 1 + 127, 0) - down, 1)
    scale = np.exp2(byte - 127.0)
    codes = (blocks / scale).astype(np.float32).astype(dtype).astype(np.float64)
    return np.moveaxis((codes * scale).reshape(v.shape), -1, axis)


WIDE = False


def mx_kscale(k):
    if not WIDE:
        return np.ones(k)
    levels = np.array([10, -10, 5, -5, 0])
    if k % 512:
        return np.exp2(np.random.permutation(np.resize(levels, k // 32))).repeat(32)
    a = np.empty((k // 512, 16))
    for p in range(k // 512):
        a[p, :8] = np.random.permutation(np.resize(levels, 8))
        for g in range(8):
            far = levels[np.abs(levels - a[p, g]) >= 10]
            a[p, g + 8] = far[np.random.randint(len(far))]
    return np.exp2(a.ravel()).repeat(32)


BF16 = ml_dtypes.bfloat16


def bf(x):
    return np.asarray(x, np.float32).astype(BF16)


def f64(x):
    return np.asarray(x).astype(np.float64)


E2M1 = np.array([0.0, 0.5, 1.0, 1.5, 2.0, 3.0, 4.0, 6.0, -0.0, -0.5, -1.0, -1.5, -2.0, -3.0, -4.0, -6.0])


def pack_weight(w, fmt):
    k, n = w.shape
    w = f64(bf(w)).reshape(k // 32, 32, n)
    amax = np.abs(w).max(1)
    if fmt == "e4m3":
        byte = np.frexp(amax)[1] - 1 + 127 - 7
    else:
        mant, ex = np.frexp(amax / 6.0)
        byte = np.where(mant > 0.5, ex, ex - 1) + 127
    byte = np.clip(np.where(amax > 0, byte, 1), 1, 254)
    scaled = (w * np.exp2(127.0 - byte)[:, None, :]).reshape(k, n).astype(np.float32)
    by_word = np.ascontiguousarray(scaled.reshape(k // 512, 128, 4, n).transpose(0, 1, 3, 2))
    if fmt == "e4m3":
        words = by_word.astype(ml_dtypes.float8_e4m3fn).view(np.uint8)
    else:
        c = by_word.astype(ml_dtypes.float4_e2m1fn).view(np.uint8) & 0xF
        words = c[..., 0::2] | (c[..., 1::2] << 4)
    return np.ascontiguousarray(words), np.ascontiguousarray(byte.astype(np.uint8).reshape(k // 512, 16, n))


def unpack_weight(words, scales, fmt):
    g, p, n, _ = words.shape
    if fmt == "e4m3":
        vals = np.ascontiguousarray(words).view(ml_dtypes.float8_e4m3fn).astype(np.float64)
    else:
        nib = np.empty((g, p, n, 4), np.uint8)
        nib[..., 0::2] = words & 0xF
        nib[..., 1::2] = words >> 4
        vals = E2M1[nib]
    vals = vals * np.repeat(np.exp2(scales.astype(np.float64) - 127.0), 8, axis=1)[..., None]
    return vals.transpose(0, 1, 3, 2).reshape(g * 512, n)
def pack4(w):
    words, scales = pack_weight(w, "e2m1")
    return words.reshape(words.shape[0], 128, -1), scales


def unpack4(words, scales):
    return unpack_weight(words.reshape(words.shape[0], 128, -1, 2), scales, "e2m1")


N, E, HD, H1, H3, DM = 1024, 8192, 256, 1024, 128, 1024
C = 2 * HD


def draw0():
    s = mx_kscale(N)
    t = mx_kscale(C)
    r = np.concatenate([np.full(HD, 2.0 / np.sqrt(HD)), np.full(HD, 8.0 / np.sqrt(N * HD))])
    H_A = bf(np.random.standard_normal((N, E)) * 0.25 * s[:, None])
    H_mean_A = bf(np.random.standard_normal((N, HD)) * 0.35 / s[:, None] * t[HD:])
    H_mean_M = bf(np.random.standard_normal((E, HD)) * 0.35 * t[:HD])
    words, scales = pack4(np.random.standard_normal((C, H3)) * (r / t)[:, None])
    return {
        "H_A": H_A,
        "H_mean_A": H_mean_A,
        "H_mean_M": H_mean_M,
        "wEA1_words": words,
        "wEA1_scales": scales,
        "bEA1": bf(np.random.standard_normal(H3) * 0.1),
    }


def core(H_A, H_mean_A, H_mean_M, wEA1_words, wEA1_scales, bEA1):
    sum_A = mxq(f64(H_A), 0, "e4m3").T @ mxq(f64(H_mean_A), 0, "e4m3")
    EventA = np.concatenate([f64(H_mean_M), sum_A], axis=1)
    return np.maximum((mxq(EventA, 1, "e4m3") @ unpack4(wEA1_words, wEA1_scales)) + f64(bEA1), 0.0)


def e4m3fn_bytes(y):
    return np.clip(np.asarray(y, np.float64), -448.0, 448.0).astype(np.float32).astype(ml_dtypes.float8_e4m3fn).view(np.uint8)


def e4m3fn_values(b):
    return np.asarray(b, np.uint8).view(ml_dtypes.float8_e4m3fn).astype(np.float64)


def setup_inputs():
    d = draw0()
    x0 = np.asarray(d['H_A']).astype(np.float64)
    s = (np.max(np.abs(x0), axis=(1,), keepdims=True) / 448.0).astype(np.float32)
    out = {}
    for k, v in d.items():
        if k == 'H_A':
            out['H_A_bytes'] = e4m3fn_bytes(x0 / s.astype(np.float64))
            out['H_A_scale'] = s
        else:
            out[k] = v
    return out


def reference(H_A_bytes, H_A_scale, H_mean_A, H_mean_M, wEA1_words, wEA1_scales, bEA1):
    return core(e4m3fn_values(H_A_bytes) * H_A_scale.astype(np.float64), H_mean_A, H_mean_M, wEA1_words, wEA1_scales, bEA1)

@@ -1,0 +1,313 @@
+from contextlib import ExitStack
+
+import concourse.mybir as mybir
+from concourse.masks import make_identity
+
+F32 = mybir.dt.float32
+BF16 = mybir.dt.bfloat16
+U32 = mybir.dt.uint32
+I32 = mybir.dt.int32
+U8 = mybir.dt.uint8
+FP8 = mybir.dt.float8_e4m3fn
+FP8X4 = mybir.dt.float8_e4m3fn_x4
+FP4X4 = mybir.dt.float4_e2m1fn_x4
+ALU = mybir.AluOpType
+COPY = mybir.ActivationFunctionType.Copy
+
+P = 128
+NODES, EVENTS, HID, OUT = 1024, 8192, 256, 128
+PASSES = NODES // 512
+QUADS = HID // 4
+CHUNKS = (256, 512, 1024, 1024, 1024, 1024, 1024, 1024, 512, 512, 256)
+V_PLANES = (4, 3, 2, 1, 2, 1, 2, 1, 1, 1, 0)
+AHEAD = 3
+
+FLOPS = 2 * NODES * EVENTS * HID + 2 * EVENTS * 2 * HID * OUT
+
+
+def tile_mymodel_icdm_pa_t_w4_kernel(tc, H_A_bytes, H_A_scale, H_mean_A, H_mean_M, wEA1_words, wEA1_scales, bEA1, out):
+    nc = tc.nc
+    n_chunks = len(CHUNKS)
+    starts = [sum(CHUNKS[:c]) for c in range(n_chunks)]
+
+    with ExitStack() as ctx:
+        keep = ctx.enter_context(tc.tile_pool(name="keep", bufs=1))
+        work = ctx.enter_context(tc.tile_pool(name="work", bufs=2))
+        psum = ctx.enter_context(tc.psum_pool(name="psum", bufs=2))
+        ctx.enter_context(tc.manual_schedule())
+
+        warm = keep.tile([P, 1], F32, name="warm")
+        nc.vector.memset(warm[:], 0.0)
+        nc.scalar.activation(out=warm[:], in_=warm[:], func=COPY)
+
+        wc = keep.tile([P, (2 * 4 * PASSES + 1) * QUADS], U32, name="wc", align_bytes=64)
+        wc_sc = keep.tile([P, (2 * 4 * PASSES + 1) * QUADS], U8, name="wc_sc", align_bytes=64)
+        nc.vector.memset(wc[:], 0)
+        nc.vector.memset(wc_sc[:].bitcast(I32), 0)
+        wq = keep.tile([P, 4, 2 * OUT], U8, name="wq", align_bytes=64)
+        wq_sc = keep.tile([P, 4, OUT], U8, name="wq_sc", align_bytes=64)
+        nc.vector.memset(wq[:].rearrange("p v b -> p (v b)").bitcast(I32), 0)
+        nc.vector.memset(wq_sc[:].rearrange("p v b -> p (v b)").bitcast(I32), 0)
+        bias_row = keep.tile([P, OUT], BF16, name="bias_row")
+        ones = keep.tile([P, P], BF16, name="ones")
+        nc.vector.memset(bias_row[:], 0.0)
+        nc.vector.memset(ones[:], 1.0)
+        ident = keep.tile([P, P], F32, name="ident")
+        make_identity(nc, ident[:])
+
+        h_scale = keep.tile([P, PASSES, 4], F32, name="h_scale")
+        nc.sync.dma_start(out=h_scale[:], in_=H_A_scale.rearrange("(g p t) o -> p g (t o)", p=P, t=4))
+
+        h_bytes = {}
+        m_rows = {}
+
+        def load_bytes(c):
+            for g in range(PASSES):
+                hb = keep.tile([P, 4, CHUNKS[c]], U8, name="hb_%d_%d" % (c, g), align_bytes=64)
+                h_bytes[c, g] = hb
+                nc.sync.dma_start(
+                    out=hb[:],
+                    in_=H_A_bytes[512 * g : 512 * (g + 1), starts[c] : starts[c] + CHUNKS[c]].rearrange("(p t) e -> p t e", t=4),
+                )
+
+        def load_rows(c):
+            m = keep.tile([P, CHUNKS[c] // P, HID], BF16, name="m_%d" % c, align_bytes=64)
+            m_rows[c] = m
+            nc.sync.dma_start(
+                out=m[:], in_=H_mean_M[starts[c] : starts[c] + CHUNKS[c], :].rearrange("(r i) k -> i r k", i=P)
+            )
+
+        load_bytes(0)
+        w_raw = keep.tile([P, PASSES, 4, HID], BF16, name="w_raw", align_bytes=64)
+        for g in range(PASSES):
+            nc.sync.dma_start(out=w_raw[:, g], in_=H_mean_A[512 * g : 512 * (g + 1), :].rearrange("(p j) c -> p j c", j=4))
+        load_bytes(1)
+        load_rows(0)
+        halves = wEA1_words[0].rearrange("(h p) b -> p h b", h=2)
+        for s in range(2):
+            nc.sync.dma_start(out=wq[64 * s : 64 * s + 64, 2 * s : 2 * s + 2, :].bitcast(I32), in_=halves.bitcast(I32))
+        q_rows = wEA1_scales[0].rearrange("(h q r) n -> q r h n", h=2, q=2)
+        for quadrant in range(4):
+            s = quadrant // 2
+            nc.sync.dma_start(
+                out=wq_sc[32 * quadrant : 32 * quadrant + 4, 2 * s : 2 * s + 2, :].bitcast(I32),
+                in_=q_rows[quadrant % 2].bitcast(I32),
+            )
+        nc.sync.dma_start(out=bias_row[0:1, :], in_=bEA1.rearrange("(o c) -> o c", o=1))
+        load_rows(1)
+        load_bytes(2)
+        load_rows(2)
+
+        bias = keep.tile([P, 4, OUT], F32, name="bias")
+
+        def make_bias():
+            pb = psum.tile([P, 4, OUT], F32, name="po", bufs=2)
+            for i in range(4):
+                nc.tensor.matmul(out=pb[:, i, :], lhsT=ones[:], rhs=bias_row[:], start=True, stop=True)
+            nc.scalar.copy(out=bias[:], in_=pb[:])
+
+        w_group = keep.tile([P, PASSES, 4, QUADS, 4], BF16, name="w_group", align_bytes=64)
+
+        def make_stationary():
+            for g in range(PASSES):
+                nc.vector.tensor_copy(out=w_group[:, g], in_=w_raw[:, g].rearrange("p j (m t) -> p t m j", t=4))
+            for g in range(PASSES):
+                for t in range(4):
+                    c0 = (2 * (4 * g + t) + 1) * QUADS
+                    nc.vector.quantize_mx(
+                        out=wc[:, c0 : c0 + QUADS].bitcast(FP8X4),
+                        scales=wc_sc[:, c0 : c0 + QUADS],
+                        in_=w_group[:, g, t].rearrange("p m j -> p (m j)"),
+                    )
+
+        wide, grouped, codes, code_sc = {}, {}, {}, {}
+        m_group, m_codes, m_sc = {}, {}, {}
+        a_group, a_codes, a_sc = {}, {}, {}
+        result = {}
+
+        def widen(c, plane):
+            g, t = divmod(plane, 4)
+            if t == 0:
+                wd = work.tile([P, 4, CHUNKS[c]], BF16, name="wide", bufs=4, align_bytes=64)
+                wide[c, g] = wd
+            dst = wide[c, g][:, t, :]
+            src = h_bytes[c, g][:, t, :].bitcast(FP8)
+            scale = h_scale[:, g, t : t + 1]
+            if plane >= 8 - V_PLANES[c]:
+                nc.vector.tensor_scalar(out=dst, in0=src, scalar1=scale, scalar2=None, op0=ALU.mult)
+            else:
+                nc.scalar.activation(out=dst, in_=src, func=COPY, scale=scale)
+
+        def interleave(c, g):
+            gr = work.tile([P, 4 * CHUNKS[c]], BF16, name="grouped", bufs=3, align_bytes=64)
+            grouped[c, g] = gr
+            nc.vector.tensor_copy(
+                out=gr[:].rearrange("p (c i t) -> p c t i", i=4, t=4),
+                in_=wide[c, g][:].rearrange("p t (c i) -> p c t i", i=4),
+            )
+
+        def quantize_h(c, g):
+            n = CHUNKS[c]
+            if g == 0:
+                cd = work.tile([P, PASSES, n], U32, name="codes", bufs=2, align_bytes=64)
+                cs = work.tile([P, PASSES, n], U8, name="code_sc", bufs=2, align_bytes=64)
+                codes[c], code_sc[c] = cd, cs
+            nc.vector.quantize_mx(out=codes[c][:, g, :].bitcast(FP8X4), scales=code_sc[c][:, g, :], in_=grouped[c, g][:])
+
+        def turn_rows(c, b):
+            n_pairs = min(2, CHUNKS[c] // 256 - 2 * b)
+            if b == 0:
+                mg = work.tile([P, 2 * CHUNKS[c]], BF16, name="m_group", bufs=2, align_bytes=64)
+                m_group[c] = mg
+            words = m_rows[c][:].rearrange("p r k -> p (r k)").bitcast(F32)
+            pt = psum.tile([P, n_pairs, 2, P], F32, name="pt", bufs=2)
+            for j in range(n_pairs):
+                w0 = 256 * (2 * b + j)
+                for u in range(2):
+                    nc.tensor.transpose(pt[:, j, u, :], words[:, w0 + u : w0 + 256 : 2], ident[:])
+            return pt, n_pairs
+
+        def empty_rows(c, b, pt, n_pairs):
+            nc.scalar.copy(
+                out=m_group[c][:].bitcast(F32)[:, 512 * b : 512 * b + 256 * n_pairs].rearrange("p (j r u) -> p j r u", r=P, u=2),
+                in_=pt[:].rearrange("p j u r -> p j r u"),
+            )
+
+        def quantize_m(c):
+            n = CHUNKS[c] // 2
+            cd = work.tile([P, n], U32, name="m_codes", bufs=3, align_bytes=64)
+            cs = work.tile([P, n], U8, name="m_sc", bufs=3, align_bytes=64)
+            m_codes[c], m_sc[c] = cd, cs
+            nc.vector.quantize_mx(out=cd[:].bitcast(FP8X4), scales=cs[:], in_=m_group[c][:])
+
+        def pool_nodes(c, j):
+            ps = psum.tile([P, 4, P], F32, name="ps", bufs=4)
+            for t in range(4):
+                for s in range(2):
+                    cols = slice(256 * j + 128 * s, 256 * j + 128 * s + 128)
+                    for g in range(PASSES):
+                        c0 = (2 * (4 * g + t) + 1 - s) * QUADS
+                        nc.tensor.matmul_mx(
+                            out=ps[:, t, :],
+                            lhsT=wc[:, c0 : c0 + P].bitcast(FP8X4),
+                            lhsT_scale=wc_sc[:, c0 : c0 + P],
+                            rhs=codes[c][:, g, cols].bitcast(FP8X4),
+                            rhs_scale=code_sc[c][:, g, cols],
+                            start=(s == 0 and g == 0),
+                            stop=(s == 1 and g == PASSES - 1),
+                        )
+            return ps
+
+        def empty_sums(c, j, ps):
+            if j == 0:
+                ag = work.tile([P, 2 * CHUNKS[c]], BF16, name="a_group", bufs=2, align_bytes=64)
+                a_group[c] = ag
+            nc.scalar.copy(
+                out=a_group[c][:, 512 * j : 512 * (j + 1)].rearrange("p (n t) -> p n t", t=4),
+                in_=ps[:].rearrange("p t n -> p n t"),
+            )
+
+        def quantize_a(c):
+            n = CHUNKS[c] // 2
+            cd = work.tile([P, n], U32, name="a_codes", bufs=2, align_bytes=64)
+            cs = work.tile([P, n], U8, name="a_sc", bufs=2, align_bytes=64)
+            a_codes[c], a_sc[c] = cd, cs
+            nc.vector.quantize_mx(out=cd[:].bitcast(FP8X4), scales=cs[:], in_=a_group[c][:])
+
+        def project(c, b):
+            n_tiles = min(4, CHUNKS[c] // P - 4 * b)
+            po = psum.tile([P, n_tiles, OUT], F32, name="po", bufs=2)
+            for i in range(n_tiles):
+                pair, s = divmod(4 * b + i, 2)
+                cols = slice(128 * pair, 128 * pair + 128)
+                for v, cd, cs in ((2 * s, m_codes[c], m_sc[c]), (2 * s + 1, a_codes[c], a_sc[c])):
+                    nc.tensor.matmul_mx(
+                        out=po[:, i, :],
+                        lhsT=cd[:, cols].bitcast(FP8X4),
+                        lhsT_scale=cs[:, cols],
+                        rhs=wq[:, v, :].bitcast(FP4X4),
+                        rhs_scale=wq_sc[:, v, :],
+                        start=(v == 2 * s),
+                        stop=(v == 2 * s + 1),
+                    )
+            return po, n_tiles
+
+        def add_bias(c, b, po, n_tiles):
+            if b == 0:
+                res = work.tile([P, CHUNKS[c] // P, OUT], F32, name="result", bufs=3)
+                result[c] = res
+            nc.vector.tensor_tensor(
+                out=result[c][:, 4 * b : 4 * b + n_tiles, :], in0=po[:], in1=bias[:, 0:n_tiles, :], op=ALU.add
+            )
+
+        def relu(c):
+            nc.vector.tensor_scalar(out=result[c][:], in0=result[c][:], scalar1=0.0, scalar2=None, op0=ALU.max)
+
+        def store(c):
+            nc.sync.dma_start(
+                out=out[starts[c] : starts[c] + CHUNKS[c], :].rearrange("(r i) k -> i r k", i=P), in_=result[c][:]
+            )
+
+        for step in range(-1, n_chunks + 2):
+            c_wide, c_quant, c_pool, c_out = step + 1, step, step - 1, step - 2
+            if 0 <= step and step + AHEAD < n_chunks:
+                load_bytes(step + AHEAD)
+                load_rows(step + AHEAD)
+
+            has_quant = 0 <= c_quant < n_chunks
+            has_pool = 0 <= c_pool < n_chunks
+            has_out = 0 <= c_out < n_chunks
+            turned = []
+            if has_quant:
+                for b in range((CHUNKS[c_quant] + 511) // 512):
+                    turned.append((b,) + turn_rows(c_quant, b))
+            if step == 1:
+                make_bias()
+            if has_out:
+                quantize_a(c_out)
+            if has_quant:
+                interleave(c_quant, 0)
+
+            planes = list(range(8)) if c_wide < n_chunks else []
+            s_planes = planes[: 8 - V_PLANES[c_wide]] if planes else []
+            v_planes = planes[len(s_planes) :]
+            n_pairs = CHUNKS[c_pool] // 256 if has_pool else 0
+            pooled = []
+            outs = []
+            slots = max(n_pairs, 1)
+            done = 0
+            if has_out and n_pairs == 0:
+                outs = [(b,) + project(c_out, b) for b in range((CHUNKS[c_out] + 511) // 512)]
+            for j in range(slots):
+                if j < n_pairs:
+                    pooled.append(pool_nodes(c_pool, j))
+                if has_out and n_pairs and j == (n_pairs - 1) // 2:
+                    outs = [(b,) + project(c_out, b) for b in range((CHUNKS[c_out] + 511) // 512)]
+                upto = len(s_planes) * (j + 1) // slots
+                for plane in s_planes[done:upto]:
+                    widen(c_wide, plane)
+                done = upto
+                if turned:
+                    empty_rows(c_quant, *turned[0])
+                    turned = turned[1:]
+                if j < n_pairs:
+                    empty_sums(c_pool, j, pooled[j])
+            for item in turned:
+                empty_rows(c_quant, *item)
+
+            if has_pool:
+                quantize_m(c_pool)
+            if has_quant:
+                interleave(c_quant, 1)
+                quantize_h(c_quant, 0)
+            for item in outs:
+                add_bias(c_out, *item)
+            if has_quant:
+                quantize_h(c_quant, 1)
+            if has_out:
+                relu(c_out)
+                store(c_out)
+            if step == 0:
+                make_stationary()
+            for plane in v_planes:
+                widen(c_wide, plane)

@@ -19,8 +19,10 @@ NODES, EVENTS, HID, OUT = 1024, 8192, 256, 128
 PASSES = NODES // 512
 QUADS = HID // 4
 CHUNKS = (256, 512, 1024, 1024, 1024, 1024, 1024, 1024, 512, 512, 256)
-V_PLANES = (4, 3, 2, 1, 2, 1, 2, 1, 1, 1, 0)
-AHEAD = 3
+V_PLANES = (4, 3, 2, 1, 2, 1, 1, 1, 0, 0, 0)
+S_INTERLEAVES = ()
+S_RELUS = (9, 10,)
+AHEAD = 4
 
 FLOPS = 2 * NODES * EVENTS * HID + 2 * EVENTS * 2 * HID * OUT
 
@@ -78,11 +80,16 @@ def tile_mymodel_icdm_pa_t_w4_kernel(tc, H_A_bytes, H_A_scale, H_mean_A, H_mean_
             )
 
         load_bytes(0)
+        load_bytes(1)
+        nc.sync.dma_start(out=bias_row[0:1, :], in_=bEA1.rearrange("(o c) -> o c", o=1))
         w_raw = keep.tile([P, PASSES, 4, HID], BF16, name="w_raw", align_bytes=64)
         for g in range(PASSES):
             nc.sync.dma_start(out=w_raw[:, g], in_=H_mean_A[512 * g : 512 * (g + 1), :].rearrange("(p j) c -> p j c", j=4))
-        load_bytes(1)
         load_rows(0)
+        load_bytes(2)
+        load_rows(1)
+        load_bytes(3)
+        load_rows(2)
         halves = wEA1_words[0].rearrange("(h p) b -> p h b", h=2)
         for s in range(2):
             nc.sync.dma_start(out=wq[64 * s : 64 * s + 64, 2 * s : 2 * s + 2, :].bitcast(I32), in_=halves.bitcast(I32))
@@ -93,10 +100,7 @@ def tile_mymodel_icdm_pa_t_w4_kernel(tc, H_A_bytes, H_A_scale, H_mean_A, H_mean_
                 out=wq_sc[32 * quadrant : 32 * quadrant + 4, 2 * s : 2 * s + 2, :].bitcast(I32),
                 in_=q_rows[quadrant % 2].bitcast(I32),
             )
-        nc.sync.dma_start(out=bias_row[0:1, :], in_=bEA1.rearrange("(o c) -> o c", o=1))
-        load_rows(1)
-        load_bytes(2)
-        load_rows(2)
+        load_rows(3)
 
         bias = keep.tile([P, 4, OUT], F32, name="bias")
 
@@ -141,7 +145,8 @@ def tile_mymodel_icdm_pa_t_w4_kernel(tc, H_A_bytes, H_A_scale, H_mean_A, H_mean_
         def interleave(c, g):
             gr = work.tile([P, 4 * CHUNKS[c]], BF16, name="grouped", bufs=3, align_bytes=64)
             grouped[c, g] = gr
-            nc.vector.tensor_copy(
+            copy = nc.scalar.copy if (c, g) in S_INTERLEAVES else nc.vector.tensor_copy
+            copy(
                 out=gr[:].rearrange("p (c i t) -> p c t i", i=4, t=4),
                 in_=wide[c, g][:].rearrange("p t (c i) -> p c t i", i=4),
             )
@@ -241,7 +246,10 @@ def tile_mymodel_icdm_pa_t_w4_kernel(tc, H_A_bytes, H_A_scale, H_mean_A, H_mean_
             )
 
         def relu(c):
-            nc.vector.tensor_scalar(out=result[c][:], in0=result[c][:], scalar1=0.0, scalar2=None, op0=ALU.max)
+            if c in S_RELUS:
+                nc.scalar.activation(out=result[c][:], in_=result[c][:], func=mybir.ActivationFunctionType.Relu)
+            else:
+                nc.vector.tensor_scalar(out=result[c][:], in0=result[c][:], scalar1=0.0, scalar2=None, op0=ALU.max)
 
         def store(c):
             nc.sync.dma_start(
@@ -257,33 +265,25 @@ def tile_mymodel_icdm_pa_t_w4_kernel(tc, H_A_bytes, H_A_scale, H_mean_A, H_mean_
             has_quant = 0 <= c_quant < n_chunks
             has_pool = 0 <= c_pool < n_chunks
             has_out = 0 <= c_out < n_chunks
+            if step == 1:
+                make_bias()
             turned = []
             if has_quant:
                 for b in range((CHUNKS[c_quant] + 511) // 512):
                     turned.append((b,) + turn_rows(c_quant, b))
-            if step == 1:
-                make_bias()
-            if has_out:
-                quantize_a(c_out)
-            if has_quant:
-                interleave(c_quant, 0)
-
             planes = list(range(8)) if c_wide < n_chunks else []
             s_planes = planes[: 8 - V_PLANES[c_wide]] if planes else []
             v_planes = planes[len(s_planes) :]
             n_pairs = CHUNKS[c_pool] // 256 if has_pool else 0
-            pooled = []
-            outs = []
             slots = max(n_pairs, 1)
+            if has_quant:
+                interleave(c_quant, 0)
+            if has_pool:
+                quantize_m(c_pool)
             done = 0
-            if has_out and n_pairs == 0:
-                outs = [(b,) + project(c_out, b) for b in range((CHUNKS[c_out] + 511) // 512)]
             for j in range(slots):
-                if j < n_pairs:
-                    pooled.append(pool_nodes(c_pool, j))
-                if has_out and n_pairs and j == (n_pairs - 1) // 2:
-                    outs = [(b,) + project(c_out, b) for b in range((CHUNKS[c_out] + 511) // 512)]
-                upto = len(s_planes) * (j + 1) // slots
+                ps = pool_nodes(c_pool, j) if j < n_pairs else None
+                upto = min(len(s_planes), -(-len(s_planes) * (j + 1) // slots))
                 for plane in s_planes[done:upto]:
                     widen(c_wide, plane)
                 done = upto
@@ -291,23 +291,25 @@ def tile_mymodel_icdm_pa_t_w4_kernel(tc, H_A_bytes, H_A_scale, H_mean_A, H_mean_
                     empty_rows(c_quant, *turned[0])
                     turned = turned[1:]
                 if j < n_pairs:
-                    empty_sums(c_pool, j, pooled[j])
+                    empty_sums(c_pool, j, ps)
             for item in turned:
                 empty_rows(c_quant, *item)
-
-            if has_pool:
-                quantize_m(c_pool)
             if has_quant:
                 interleave(c_quant, 1)
+            outs = []
+            if has_out:
+                quantize_a(c_out)
+                outs = [(b,) + project(c_out, b) for b in range((CHUNKS[c_out] + 511) // 512)]
+            if has_quant:
                 quantize_h(c_quant, 0)
-            for item in outs:
-                add_bias(c_out, *item)
             if has_quant:
                 quantize_h(c_quant, 1)
-            if has_out:
-                relu(c_out)
-                store(c_out)
             if step == 0:
                 make_stationary()
             for plane in v_planes:
                 widen(c_wide, plane)
+            for item in outs:
+                add_bias(c_out, *item)
+            if has_out:
+                relu(c_out)
+                store(c_out)

@@ -19,9 +19,10 @@ NODES, EVENTS, HID, OUT = 1024, 8192, 256, 128
 PASSES = NODES // 512
 QUADS = HID // 4
 CHUNKS = (256, 512, 1024, 1024, 1024, 1024, 1024, 1024, 512, 512, 256)
-V_PLANES = (4, 3, 2, 1, 2, 1, 1, 1, 0, 0, 0)
-S_INTERLEAVES = ()
-S_RELUS = (9, 10,)
+V_PLANES = (5, 2, 2, 3, 3, 3, 2, 2, 0, 1, 2)
+PE_BLOCKS = (0, 0, 0, 2, 2, 2, 2, 2, 0, 1, 0)
+S_INTERLEAVES = ((9, 1), (10, 1),)
+S_RELUS = (8,)
 AHEAD = 4
 
 FLOPS = 2 * NODES * EVENTS * HID + 2 * EVENTS * 2 * HID * OUT
@@ -36,7 +37,7 @@ def tile_mymodel_icdm_pa_t_w4_kernel(tc, H_A_bytes, H_A_scale, H_mean_A, H_mean_
         keep = ctx.enter_context(tc.tile_pool(name="keep", bufs=1))
         work = ctx.enter_context(tc.tile_pool(name="work", bufs=2))
         psum = ctx.enter_context(tc.psum_pool(name="psum", bufs=2))
-        ctx.enter_context(tc.manual_schedule())
+        ctx.enter_context(tc.manual_schedule(engines={mybir.EngineType.SP}))
 
         warm = keep.tile([P, 1], F32, name="warm")
         nc.vector.memset(warm[:], 0.0)
@@ -56,6 +57,9 @@ def tile_mymodel_icdm_pa_t_w4_kernel(tc, H_A_bytes, H_A_scale, H_mean_A, H_mean_
         nc.vector.memset(ones[:], 1.0)
         ident = keep.tile([P, P], F32, name="ident")
         make_identity(nc, ident[:])
+
+        ident_bf = keep.tile([P, P], BF16, name="ident_bf")
+        make_identity(nc, ident_bf[:])
 
         h_scale = keep.tile([P, PASSES, 4], F32, name="h_scale")
         nc.sync.dma_start(out=h_scale[:], in_=H_A_scale.rearrange("(g p t) o -> p g (t o)", p=P, t=4))
@@ -145,11 +149,29 @@ def tile_mymodel_icdm_pa_t_w4_kernel(tc, H_A_bytes, H_A_scale, H_mean_A, H_mean_
         def interleave(c, g):
             gr = work.tile([P, 4 * CHUNKS[c]], BF16, name="grouped", bufs=3, align_bytes=64)
             grouped[c, g] = gr
+            first = 256 * PE_BLOCKS[c] if g == 1 else 0
             copy = nc.scalar.copy if (c, g) in S_INTERLEAVES else nc.vector.tensor_copy
-            copy(
-                out=gr[:].rearrange("p (c i t) -> p c t i", i=4, t=4),
-                in_=wide[c, g][:].rearrange("p t (c i) -> p c t i", i=4),
-            )
+            if first < CHUNKS[c]:
+                copy(
+                    out=gr[:, 4 * first :].rearrange("p (c i t) -> p c t i", i=4, t=4),
+                    in_=wide[c, g][:, :, first:].rearrange("p t (c i) -> p c t i", i=4),
+                )
+
+        def weave(c, b):
+            pf = psum.tile([P, 1024], BF16, name="pf", bufs=1)
+            for h in range(2):
+                e0 = 256 * b + 128 * h
+                nc.tensor.matmul(
+                    out=pf[:, 512 * h : 512 * (h + 1)],
+                    lhsT=ident_bf[:],
+                    rhs=wide[c, 1][:, :, e0 : e0 + 128].rearrange("p t e -> p e t"),
+                    start=True,
+                    stop=True,
+                )
+            return pf
+
+        def empty_woven(c, b, pf):
+            nc.scalar.copy(out=grouped[c, 1][:, 1024 * b : 1024 * (b + 1)], in_=pf[:])
 
         def quantize_h(c, g):
             n = CHUNKS[c]
@@ -186,7 +208,7 @@ def tile_mymodel_icdm_pa_t_w4_kernel(tc, H_A_bytes, H_A_scale, H_mean_A, H_mean_
             nc.vector.quantize_mx(out=cd[:].bitcast(FP8X4), scales=cs[:], in_=m_group[c][:])
 
         def pool_nodes(c, j):
-            ps = psum.tile([P, 4, P], F32, name="ps", bufs=4)
+            ps = psum.tile([P, 4, P], F32, name="ps", bufs=3)
             for t in range(4):
                 for s in range(2):
                     cols = slice(256 * j + 128 * s, 256 * j + 128 * s + 128)
@@ -278,15 +300,20 @@ def tile_mymodel_icdm_pa_t_w4_kernel(tc, H_A_bytes, H_A_scale, H_mean_A, H_mean_
             slots = max(n_pairs, 1)
             if has_quant:
                 interleave(c_quant, 0)
-            if has_pool:
-                quantize_m(c_pool)
+            if has_quant:
+                interleave(c_quant, 1)
+            n_woven = PE_BLOCKS[c_quant] if has_quant else 0
+            slots = max(slots, n_woven)
             done = 0
             for j in range(slots):
+                pf = weave(c_quant, j) if j < n_woven else None
                 ps = pool_nodes(c_pool, j) if j < n_pairs else None
                 upto = min(len(s_planes), -(-len(s_planes) * (j + 1) // slots))
                 for plane in s_planes[done:upto]:
                     widen(c_wide, plane)
                 done = upto
+                if j < n_woven:
+                    empty_woven(c_quant, j, pf)
                 if turned:
                     empty_rows(c_quant, *turned[0])
                     turned = turned[1:]
@@ -294,8 +321,8 @@ def tile_mymodel_icdm_pa_t_w4_kernel(tc, H_A_bytes, H_A_scale, H_mean_A, H_mean_
                     empty_sums(c_pool, j, ps)
             for item in turned:
                 empty_rows(c_quant, *item)
-            if has_quant:
-                interleave(c_quant, 1)
+            if has_pool:
+                quantize_m(c_pool)
             outs = []
             if has_out:
                 quantize_a(c_out)

@@ -13,25 +13,33 @@ FP8X4 = mybir.dt.float8_e4m3fn_x4
 FP4X4 = mybir.dt.float4_e2m1fn_x4
 ALU = mybir.AluOpType
 COPY = mybir.ActivationFunctionType.Copy
+RELU = mybir.ActivationFunctionType.Relu
+
+NODES, EVENTS, HIDDEN, OUT = 1024, 8192, 256, 128
 
 P = 128
-NODES, EVENTS, HID, OUT = 1024, 8192, 256, 128
-PASSES = NODES // 512
-QUADS = HID // 4
+PACK = 4
+PASS = P * PACK
+GROUPS = NODES // PASS
+PAIR = 2 * P
+QUADS = HIDDEN // PACK
+BANK = 512
+PLANES = GROUPS * PACK
+
 CHUNKS = (256, 512, 1024, 1024, 1024, 1024, 1024, 1024, 512, 512, 256)
-V_PLANES = (5, 2, 2, 3, 3, 3, 2, 2, 0, 1, 2)
-PE_BLOCKS = (0, 0, 0, 2, 2, 2, 2, 2, 0, 1, 0)
-S_INTERLEAVES = ((9, 1), (10, 1),)
-S_RELUS = (8,)
+VECTOR_PLANES = (5, 2, 3, 3, 4, 4, 4, 3, 1, 4, 0)
+FIRST_DIRECT = 7
 AHEAD = 4
 
-FLOPS = 2 * NODES * EVENTS * HID + 2 * EVENTS * 2 * HID * OUT
+FLOPS = 2 * NODES * EVENTS * HIDDEN + 2 * EVENTS * 2 * HIDDEN * OUT
 
 
-def tile_mymodel_icdm_pa_t_w4_kernel(tc, H_A_bytes, H_A_scale, H_mean_A, H_mean_M, wEA1_words, wEA1_scales, bEA1, out):
+def tile_mymodel_icdm_pa_t_w4_kernel(
+    tc, H_A_bytes, H_A_scale, H_mean_A, H_mean_M, wEA1_words, wEA1_scales, bEA1, out
+):
     nc = tc.nc
     n_chunks = len(CHUNKS)
-    starts = [sum(CHUNKS[:c]) for c in range(n_chunks)]
+    first_event = [sum(CHUNKS[:c]) for c in range(n_chunks)]
 
     with ExitStack() as ctx:
         keep = ctx.enter_context(tc.tile_pool(name="keep", bufs=1))
@@ -43,300 +51,284 @@ def tile_mymodel_icdm_pa_t_w4_kernel(tc, H_A_bytes, H_A_scale, H_mean_A, H_mean_
         nc.vector.memset(warm[:], 0.0)
         nc.scalar.activation(out=warm[:], in_=warm[:], func=COPY)
 
-        wc = keep.tile([P, (2 * 4 * PASSES + 1) * QUADS], U32, name="wc", align_bytes=64)
-        wc_sc = keep.tile([P, (2 * 4 * PASSES + 1) * QUADS], U8, name="wc_sc", align_bytes=64)
-        nc.vector.memset(wc[:], 0)
-        nc.vector.memset(wc_sc[:].bitcast(I32), 0)
-        wq = keep.tile([P, 4, 2 * OUT], U8, name="wq", align_bytes=64)
-        wq_sc = keep.tile([P, 4, OUT], U8, name="wq_sc", align_bytes=64)
-        nc.vector.memset(wq[:].rearrange("p v b -> p (v b)").bitcast(I32), 0)
-        nc.vector.memset(wq_sc[:].rearrange("p v b -> p (v b)").bitcast(I32), 0)
+
+        n_blocks = 2 * PLANES + 1
+        node_codes = keep.tile([P, n_blocks * QUADS], U32, name="node_codes", align_bytes=64)
+        node_scales = keep.tile([P, n_blocks * QUADS], U8, name="node_scales", align_bytes=64)
+        nc.vector.memset(node_codes[:], 0)
+        nc.vector.memset(node_scales[:].bitcast(I32), 0)
+
+        weight = keep.tile([P, 4, 2 * OUT], U8, name="weight", align_bytes=64)
+        weight_scales = keep.tile([P, 4, OUT], U8, name="weight_scales", align_bytes=64)
+        nc.vector.memset(weight[:].rearrange("p v b -> p (v b)").bitcast(I32), 0)
+        nc.vector.memset(weight_scales[:].rearrange("p v n -> p (v n)").bitcast(I32), 0)
+
+        bias_in = keep.tile([P, 1], BF16, name="bias_in")
+        bias_column = keep.tile([P, 1], F32, name="bias_column")
         bias_row = keep.tile([P, OUT], BF16, name="bias_row")
+        bias_spread = keep.tile([P, BANK // OUT, OUT], F32, name="bias_spread")
         ones = keep.tile([P, P], BF16, name="ones")
         nc.vector.memset(bias_row[:], 0.0)
         nc.vector.memset(ones[:], 1.0)
-        ident = keep.tile([P, P], F32, name="ident")
-        make_identity(nc, ident[:])
+        identity = keep.tile([P, P], F32, name="identity")
+        make_identity(nc, identity[:])
 
-        ident_bf = keep.tile([P, P], BF16, name="ident_bf")
-        make_identity(nc, ident_bf[:])
 
-        h_scale = keep.tile([P, PASSES, 4], F32, name="h_scale")
-        nc.sync.dma_start(out=h_scale[:], in_=H_A_scale.rearrange("(g p t) o -> p g (t o)", p=P, t=4))
+        plane_scales = keep.tile([P, GROUPS, PACK], F32, name="plane_scales")
+        nc.sync.dma_start(out=plane_scales[:], in_=H_A_scale.rearrange("(g p t) o -> p g (t o)", p=P, t=PACK))
 
-        h_bytes = {}
-        m_rows = {}
+        event_bytes = {}
+        event_rows = {}
 
         def load_bytes(c):
-            for g in range(PASSES):
-                hb = keep.tile([P, 4, CHUNKS[c]], U8, name="hb_%d_%d" % (c, g), align_bytes=64)
-                h_bytes[c, g] = hb
-                nc.sync.dma_start(
-                    out=hb[:],
-                    in_=H_A_bytes[512 * g : 512 * (g + 1), starts[c] : starts[c] + CHUNKS[c]].rearrange("(p t) e -> p t e", t=4),
-                )
+            events = slice(first_event[c], first_event[c] + CHUNKS[c])
+            for g in range(GROUPS):
+                raw = keep.tile([P, PACK, CHUNKS[c]], U8, name="bytes_%d_%d" % (c, g), align_bytes=64)
+                event_bytes[c, g] = raw
+                nodes = slice(PASS * g, PASS * (g + 1))
+                nc.sync.dma_start(out=raw[:], in_=H_A_bytes[nodes, events].rearrange("(p t) e -> p t e", t=PACK))
 
         def load_rows(c):
-            m = keep.tile([P, CHUNKS[c] // P, HID], BF16, name="m_%d" % c, align_bytes=64)
-            m_rows[c] = m
-            nc.sync.dma_start(
-                out=m[:], in_=H_mean_M[starts[c] : starts[c] + CHUNKS[c], :].rearrange("(r i) k -> i r k", i=P)
-            )
+            events = slice(first_event[c], first_event[c] + CHUNKS[c])
+            rows = keep.tile([P, CHUNKS[c] // P, HIDDEN], BF16, name="rows_%d" % c, align_bytes=64)
+            event_rows[c] = rows
+            nc.sync.dma_start(out=rows[:], in_=H_mean_M[events, :].rearrange("(r i) k -> i r k", i=P))
 
         load_bytes(0)
         load_bytes(1)
+        nc.sync.dma_start(out=bias_in[:], in_=bEA1.rearrange("(c o) -> c o", o=1))
         nc.sync.dma_start(out=bias_row[0:1, :], in_=bEA1.rearrange("(o c) -> o c", o=1))
-        w_raw = keep.tile([P, PASSES, 4, HID], BF16, name="w_raw", align_bytes=64)
-        for g in range(PASSES):
-            nc.sync.dma_start(out=w_raw[:, g], in_=H_mean_A[512 * g : 512 * (g + 1), :].rearrange("(p j) c -> p j c", j=4))
+        node_rows = keep.tile([P, GROUPS, PACK, HIDDEN], BF16, name="node_rows", align_bytes=64)
+        for g in range(GROUPS):
+            nodes = slice(PASS * g, PASS * (g + 1))
+            nc.sync.dma_start(out=node_rows[:, g], in_=H_mean_A[nodes, :].rearrange("(p j) c -> p j c", j=PACK))
         load_rows(0)
         load_bytes(2)
         load_rows(1)
         load_bytes(3)
         load_rows(2)
-        halves = wEA1_words[0].rearrange("(h p) b -> p h b", h=2)
-        for s in range(2):
-            nc.sync.dma_start(out=wq[64 * s : 64 * s + 64, 2 * s : 2 * s + 2, :].bitcast(I32), in_=halves.bitcast(I32))
-        q_rows = wEA1_scales[0].rearrange("(h q r) n -> q r h n", h=2, q=2)
+        word_halves = wEA1_words[0].rearrange("(h p) b -> p h b", h=2).bitcast(I32)
+        scale_quadrants = wEA1_scales[0].rearrange("(h r b) n -> r b h n", h=2, r=2)
+        for side in range(2):
+            forms = slice(2 * side, 2 * side + 2)
+            nc.sync.dma_start(out=weight[QUADS * side : QUADS * (side + 1), forms, :].bitcast(I32), in_=word_halves)
         for quadrant in range(4):
-            s = quadrant // 2
+            side, r = divmod(quadrant, 2)
+            forms = slice(2 * side, 2 * side + 2)
             nc.sync.dma_start(
-                out=wq_sc[32 * quadrant : 32 * quadrant + 4, 2 * s : 2 * s + 2, :].bitcast(I32),
-                in_=q_rows[quadrant % 2].bitcast(I32),
+                out=weight_scales[32 * quadrant : 32 * quadrant + 4, forms, :].bitcast(I32),
+                in_=scale_quadrants[r].bitcast(I32),
             )
         load_rows(3)
 
-        bias = keep.tile([P, 4, OUT], F32, name="bias")
 
-        def make_bias():
-            pb = psum.tile([P, 4, OUT], F32, name="po", bufs=2)
-            for i in range(4):
-                nc.tensor.matmul(out=pb[:, i, :], lhsT=ones[:], rhs=bias_row[:], start=True, stop=True)
-            nc.scalar.copy(out=bias[:], in_=pb[:])
+        def spread_bias():
+            po = psum.tile([P, BANK // OUT, OUT], F32, name="po", bufs=2)
+            for i in range(BANK // OUT):
+                nc.tensor.matmul(out=po[:, i, :], lhsT=ones[:], rhs=bias_row[:], start=True, stop=True)
+            nc.scalar.copy(out=bias_spread[:], in_=po[:])
+            nc.scalar.copy(out=bias_column[:], in_=bias_in[:])
 
-        w_group = keep.tile([P, PASSES, 4, QUADS, 4], BF16, name="w_group", align_bytes=64)
-
-        def make_stationary():
-            for g in range(PASSES):
-                nc.vector.tensor_copy(out=w_group[:, g], in_=w_raw[:, g].rearrange("p j (m t) -> p t m j", t=4))
-            for g in range(PASSES):
-                for t in range(4):
-                    c0 = (2 * (4 * g + t) + 1) * QUADS
+        def quantize_nodes():
+            grouped = keep.tile([P, GROUPS, PACK, QUADS, PACK], BF16, name="node_grouped", align_bytes=64)
+            for g in range(GROUPS):
+                nc.vector.tensor_copy(out=grouped[:, g], in_=node_rows[:, g].rearrange("p j (q t) -> p t q j", t=PACK))
+            for g in range(GROUPS):
+                for t in range(PACK):
+                    c0 = (2 * (PACK * g + t) + 1) * QUADS
                     nc.vector.quantize_mx(
-                        out=wc[:, c0 : c0 + QUADS].bitcast(FP8X4),
-                        scales=wc_sc[:, c0 : c0 + QUADS],
-                        in_=w_group[:, g, t].rearrange("p m j -> p (m j)"),
+                        out=node_codes[:, c0 : c0 + QUADS].bitcast(FP8X4),
+                        scales=node_scales[:, c0 : c0 + QUADS],
+                        in_=grouped[:, g, t].rearrange("p q j -> p (q j)"),
                     )
 
-        wide, grouped, codes, code_sc = {}, {}, {}, {}
-        m_group, m_codes, m_sc = {}, {}, {}
-        a_group, a_codes, a_sc = {}, {}, {}
-        result = {}
+
+        wide, h_grouped, h_codes, h_scales = {}, {}, {}, {}
+        m_grouped, m_codes, m_scales = {}, {}, {}
+        a_grouped, a_codes, a_scales = {}, {}, {}
+        results = {}
 
         def widen(c, plane):
-            g, t = divmod(plane, 4)
+            g, t = divmod(plane, PACK)
             if t == 0:
-                wd = work.tile([P, 4, CHUNKS[c]], BF16, name="wide", bufs=4, align_bytes=64)
-                wide[c, g] = wd
-            dst = wide[c, g][:, t, :]
-            src = h_bytes[c, g][:, t, :].bitcast(FP8)
-            scale = h_scale[:, g, t : t + 1]
-            if plane >= 8 - V_PLANES[c]:
-                nc.vector.tensor_scalar(out=dst, in0=src, scalar1=scale, scalar2=None, op0=ALU.mult)
+                planes = work.tile([P, PACK, CHUNKS[c]], BF16, name="wide", bufs=4, align_bytes=64)
+                wide[c, g] = planes
+            values = event_bytes[c, g][:, t, :].bitcast(FP8)
+            scale = plane_scales[:, g, t : t + 1]
+            if plane < PLANES - VECTOR_PLANES[c]:
+                nc.scalar.activation(out=wide[c, g][:, t, :], in_=values, func=COPY, scale=scale)
             else:
-                nc.scalar.activation(out=dst, in_=src, func=COPY, scale=scale)
+                nc.vector.tensor_scalar(
+                    out=wide[c, g][:, t, :], in0=values, scalar1=scale, scalar2=None, op0=ALU.mult
+                )
 
         def interleave(c, g):
-            gr = work.tile([P, 4 * CHUNKS[c]], BF16, name="grouped", bufs=3, align_bytes=64)
-            grouped[c, g] = gr
-            first = 256 * PE_BLOCKS[c] if g == 1 else 0
-            copy = nc.scalar.copy if (c, g) in S_INTERLEAVES else nc.vector.tensor_copy
-            if first < CHUNKS[c]:
-                copy(
-                    out=gr[:, 4 * first :].rearrange("p (c i t) -> p c t i", i=4, t=4),
-                    in_=wide[c, g][:, :, first:].rearrange("p t (c i) -> p c t i", i=4),
-                )
-
-        def weave(c, b):
-            pf = psum.tile([P, 1024], BF16, name="pf", bufs=1)
-            for h in range(2):
-                e0 = 256 * b + 128 * h
-                nc.tensor.matmul(
-                    out=pf[:, 512 * h : 512 * (h + 1)],
-                    lhsT=ident_bf[:],
-                    rhs=wide[c, 1][:, :, e0 : e0 + 128].rearrange("p t e -> p e t"),
-                    start=True,
-                    stop=True,
-                )
-            return pf
-
-        def empty_woven(c, b, pf):
-            nc.scalar.copy(out=grouped[c, 1][:, 1024 * b : 1024 * (b + 1)], in_=pf[:])
-
-        def quantize_h(c, g):
-            n = CHUNKS[c]
-            if g == 0:
-                cd = work.tile([P, PASSES, n], U32, name="codes", bufs=2, align_bytes=64)
-                cs = work.tile([P, PASSES, n], U8, name="code_sc", bufs=2, align_bytes=64)
-                codes[c], code_sc[c] = cd, cs
-            nc.vector.quantize_mx(out=codes[c][:, g, :].bitcast(FP8X4), scales=code_sc[c][:, g, :], in_=grouped[c, g][:])
-
-        def turn_rows(c, b):
-            n_pairs = min(2, CHUNKS[c] // 256 - 2 * b)
-            if b == 0:
-                mg = work.tile([P, 2 * CHUNKS[c]], BF16, name="m_group", bufs=2, align_bytes=64)
-                m_group[c] = mg
-            words = m_rows[c][:].rearrange("p r k -> p (r k)").bitcast(F32)
-            pt = psum.tile([P, n_pairs, 2, P], F32, name="pt", bufs=2)
-            for j in range(n_pairs):
-                w0 = 256 * (2 * b + j)
-                for u in range(2):
-                    nc.tensor.transpose(pt[:, j, u, :], words[:, w0 + u : w0 + 256 : 2], ident[:])
-            return pt, n_pairs
-
-        def empty_rows(c, b, pt, n_pairs):
-            nc.scalar.copy(
-                out=m_group[c][:].bitcast(F32)[:, 512 * b : 512 * b + 256 * n_pairs].rearrange("p (j r u) -> p j r u", r=P, u=2),
-                in_=pt[:].rearrange("p j u r -> p j r u"),
+            grouped = work.tile([P, PACK * CHUNKS[c]], BF16, name="h_grouped", bufs=3, align_bytes=64)
+            h_grouped[c, g] = grouped
+            nc.vector.tensor_copy(
+                out=grouped[:].rearrange("p (e i t) -> p e t i", i=4, t=PACK),
+                in_=wide[c, g][:].rearrange("p t (e i) -> p e t i", i=4),
             )
 
-        def quantize_m(c):
-            n = CHUNKS[c] // 2
-            cd = work.tile([P, n], U32, name="m_codes", bufs=3, align_bytes=64)
-            cs = work.tile([P, n], U8, name="m_sc", bufs=3, align_bytes=64)
-            m_codes[c], m_sc[c] = cd, cs
-            nc.vector.quantize_mx(out=cd[:].bitcast(FP8X4), scales=cs[:], in_=m_group[c][:])
+        def quantize_events(c, g):
+            if g == 0:
+                codes = work.tile([P, GROUPS, CHUNKS[c]], U32, name="h_codes", bufs=2, align_bytes=64)
+                scales = work.tile([P, GROUPS, CHUNKS[c]], U8, name="h_scales", bufs=2, align_bytes=64)
+                h_codes[c], h_scales[c] = codes, scales
+            nc.vector.quantize_mx(
+                out=h_codes[c][:, g, :].bitcast(FP8X4), scales=h_scales[c][:, g, :], in_=h_grouped[c, g][:]
+            )
 
         def pool_nodes(c, j):
-            ps = psum.tile([P, 4, P], F32, name="ps", bufs=3)
-            for t in range(4):
-                for s in range(2):
-                    cols = slice(256 * j + 128 * s, 256 * j + 128 * s + 128)
-                    for g in range(PASSES):
-                        c0 = (2 * (4 * g + t) + 1 - s) * QUADS
+            ps = psum.tile([P, PACK, P], F32, name="ps", bufs=2)
+            for t in range(PACK):
+                for side in range(2):
+                    cols = slice(PAIR * j + P * side, PAIR * j + P * (side + 1))
+                    for g in range(GROUPS):
+                        c0 = (2 * (PACK * g + t) + 1 - side) * QUADS
                         nc.tensor.matmul_mx(
                             out=ps[:, t, :],
-                            lhsT=wc[:, c0 : c0 + P].bitcast(FP8X4),
-                            lhsT_scale=wc_sc[:, c0 : c0 + P],
-                            rhs=codes[c][:, g, cols].bitcast(FP8X4),
-                            rhs_scale=code_sc[c][:, g, cols],
-                            start=(s == 0 and g == 0),
-                            stop=(s == 1 and g == PASSES - 1),
+                            lhsT=node_codes[:, c0 : c0 + P].bitcast(FP8X4),
+                            lhsT_scale=node_scales[:, c0 : c0 + P],
+                            rhs=h_codes[c][:, g, cols].bitcast(FP8X4),
+                            rhs_scale=h_scales[c][:, g, cols],
+                            start=(side == 0 and g == 0),
+                            stop=(side == 1 and g == GROUPS - 1),
                         )
             return ps
 
         def empty_sums(c, j, ps):
             if j == 0:
-                ag = work.tile([P, 2 * CHUNKS[c]], BF16, name="a_group", bufs=2, align_bytes=64)
-                a_group[c] = ag
+                grouped = work.tile([P, PACK * CHUNKS[c] // 2], BF16, name="a_grouped", bufs=2, align_bytes=64)
+                a_grouped[c] = grouped
             nc.scalar.copy(
-                out=a_group[c][:, 512 * j : 512 * (j + 1)].rearrange("p (n t) -> p n t", t=4),
+                out=a_grouped[c][:, BANK * j : BANK * (j + 1)].rearrange("p (n t) -> p n t", t=PACK),
                 in_=ps[:].rearrange("p t n -> p n t"),
             )
 
-        def quantize_a(c):
-            n = CHUNKS[c] // 2
-            cd = work.tile([P, n], U32, name="a_codes", bufs=2, align_bytes=64)
-            cs = work.tile([P, n], U8, name="a_sc", bufs=2, align_bytes=64)
-            a_codes[c], a_sc[c] = cd, cs
-            nc.vector.quantize_mx(out=cd[:].bitcast(FP8X4), scales=cs[:], in_=a_group[c][:])
-
-        def project(c, b):
-            n_tiles = min(4, CHUNKS[c] // P - 4 * b)
-            po = psum.tile([P, n_tiles, OUT], F32, name="po", bufs=2)
-            for i in range(n_tiles):
-                pair, s = divmod(4 * b + i, 2)
-                cols = slice(128 * pair, 128 * pair + 128)
-                for v, cd, cs in ((2 * s, m_codes[c], m_sc[c]), (2 * s + 1, a_codes[c], a_sc[c])):
-                    nc.tensor.matmul_mx(
-                        out=po[:, i, :],
-                        lhsT=cd[:, cols].bitcast(FP8X4),
-                        lhsT_scale=cs[:, cols],
-                        rhs=wq[:, v, :].bitcast(FP4X4),
-                        rhs_scale=wq_sc[:, v, :],
-                        start=(v == 2 * s),
-                        stop=(v == 2 * s + 1),
-                    )
-            return po, n_tiles
-
-        def add_bias(c, b, po, n_tiles):
+        def turn_rows(c, b):
+            n_pairs = min(2, CHUNKS[c] // PAIR - 2 * b)
             if b == 0:
-                res = work.tile([P, CHUNKS[c] // P, OUT], F32, name="result", bufs=3)
-                result[c] = res
-            nc.vector.tensor_tensor(
-                out=result[c][:, 4 * b : 4 * b + n_tiles, :], in0=po[:], in1=bias[:, 0:n_tiles, :], op=ALU.add
+                grouped = work.tile([P, PACK * CHUNKS[c] // 2], BF16, name="m_grouped", bufs=2, align_bytes=64)
+                m_grouped[c] = grouped
+            words = event_rows[c][:].rearrange("p r k -> p (r k)").bitcast(F32)
+            pt = psum.tile([P, n_pairs, 2, P], F32, name="pt", bufs=2)
+            for j in range(n_pairs):
+                w0 = HIDDEN * (2 * b + j)
+                for u in range(2):
+                    nc.tensor.transpose(pt[:, j, u, :], words[:, w0 + u : w0 + HIDDEN : 2], identity[:])
+            nc.scalar.copy(
+                out=m_grouped[c][:]
+                .bitcast(F32)[:, BANK * b : BANK * b + HIDDEN * n_pairs]
+                .rearrange("p (j n u) -> p j n u", n=P, u=2),
+                in_=pt[:].rearrange("p j u n -> p j n u"),
             )
 
-        def relu(c):
-            if c in S_RELUS:
-                nc.scalar.activation(out=result[c][:], in_=result[c][:], func=mybir.ActivationFunctionType.Relu)
-            else:
-                nc.vector.tensor_scalar(out=result[c][:], in0=result[c][:], scalar1=0.0, scalar2=None, op0=ALU.max)
+        def quantize_rows(c):
+            codes = work.tile([P, CHUNKS[c] // 2], U32, name="m_codes", bufs=3, align_bytes=64)
+            scales = work.tile([P, CHUNKS[c] // 2], U8, name="m_scales", bufs=3, align_bytes=64)
+            m_codes[c], m_scales[c] = codes, scales
+            nc.vector.quantize_mx(out=codes[:].bitcast(FP8X4), scales=scales[:], in_=m_grouped[c][:])
+
+        def quantize_sums(c):
+            codes = work.tile([P, CHUNKS[c] // 2], U32, name="a_codes", bufs=2, align_bytes=64)
+            scales = work.tile([P, CHUNKS[c] // 2], U8, name="a_scales", bufs=2, align_bytes=64)
+            a_codes[c], a_scales[c] = codes, scales
+            nc.vector.quantize_mx(out=codes[:].bitcast(FP8X4), scales=scales[:], in_=a_grouped[c][:])
+
+        def halves(c):
+            return ((0, m_codes[c], m_scales[c]), (1, a_codes[c], a_scales[c]))
+
+        def new_result(c):
+            result = work.tile([P, CHUNKS[c] // P, OUT], F32, name="result", bufs=3)
+            results[c] = result
+
+        def finish_direct(c):
+            new_result(c)
+            n_sets = CHUNKS[c] // P
+            for r0 in range(0, n_sets, BANK // OUT):
+                n = min(BANK // OUT, n_sets - r0)
+                po = psum.tile([P, n, OUT], F32, name="po", bufs=2)
+                for i in range(n):
+                    pair, side = divmod(r0 + i, 2)
+                    cols = slice(P * pair, P * (pair + 1))
+                    for half, codes, scales in halves(c):
+                        nc.tensor.matmul_mx(
+                            out=po[:, i, :],
+                            lhsT=codes[:, cols].bitcast(FP8X4),
+                            lhsT_scale=scales[:, cols],
+                            rhs=weight[:, 2 * side + half, :].bitcast(FP4X4),
+                            rhs_scale=weight_scales[:, 2 * side + half, :],
+                            start=(half == 0),
+                            stop=(half == 1),
+                        )
+                nc.vector.tensor_tensor(
+                    out=results[c][:, r0 : r0 + n, :], in0=po[:], in1=bias_spread[:, 0:n, :], op=ALU.add
+                )
+            nc.vector.tensor_scalar(out=results[c][:], in0=results[c][:], scalar1=0.0, scalar2=None, op0=ALU.max)
+
+        def finish_turned(c):
+            n = CHUNKS[c] // 2
+            width = BANK if n == BANK else P
+            turned = []
+            for side in range(2):
+                po = psum.tile([P, n], F32, name="po", bufs=2)
+                for c0 in range(0, n, width):
+                    cols = slice(c0, c0 + width)
+                    for half, codes, scales in halves(c):
+                        nc.tensor.matmul_mx(
+                            out=po[:, cols],
+                            lhsT=weight[:, 2 * side + half, :].bitcast(FP4X4),
+                            lhsT_scale=weight_scales[:, 2 * side + half, :],
+                            rhs=codes[:, cols].bitcast(FP8X4),
+                            rhs_scale=scales[:, cols],
+                            start=(half == 0),
+                            stop=(half == 1),
+                        )
+                channels = work.tile([P, n], F32, name="channels", bufs=2)
+                nc.scalar.activation(out=channels[:], in_=po[:], func=RELU, bias=bias_column[:])
+                turned.append(channels)
+            new_result(c)
+            for side in range(2):
+                pz = psum.tile([P, n // P, OUT], F32, name="pz", bufs=2)
+                for j in range(n // P):
+                    nc.tensor.transpose(pz[:, j, :], turned[side][:, P * j : P * (j + 1)], identity[:])
+                nc.scalar.copy(out=results[c][:, side::2, :], in_=pz[:])
 
         def store(c):
-            nc.sync.dma_start(
-                out=out[starts[c] : starts[c] + CHUNKS[c], :].rearrange("(r i) k -> i r k", i=P), in_=result[c][:]
-            )
+            events = slice(first_event[c], first_event[c] + CHUNKS[c])
+            nc.sync.dma_start(out=out[events, :].rearrange("(r i) k -> i r k", i=P), in_=results[c][:])
+
 
         for step in range(-1, n_chunks + 2):
-            c_wide, c_quant, c_pool, c_out = step + 1, step, step - 1, step - 2
-            if 0 <= step and step + AHEAD < n_chunks:
+            to_widen, to_quantize, to_pool, to_finish = step + 1, step, step - 1, step - 2
+            if 0 <= step < n_chunks - AHEAD:
                 load_bytes(step + AHEAD)
                 load_rows(step + AHEAD)
-
-            has_quant = 0 <= c_quant < n_chunks
-            has_pool = 0 <= c_pool < n_chunks
-            has_out = 0 <= c_out < n_chunks
-            if step == 1:
-                make_bias()
-            turned = []
-            if has_quant:
-                for b in range((CHUNKS[c_quant] + 511) // 512):
-                    turned.append((b,) + turn_rows(c_quant, b))
-            planes = list(range(8)) if c_wide < n_chunks else []
-            s_planes = planes[: 8 - V_PLANES[c_wide]] if planes else []
-            v_planes = planes[len(s_planes) :]
-            n_pairs = CHUNKS[c_pool] // 256 if has_pool else 0
-            slots = max(n_pairs, 1)
-            if has_quant:
-                interleave(c_quant, 0)
-            if has_quant:
-                interleave(c_quant, 1)
-            n_woven = PE_BLOCKS[c_quant] if has_quant else 0
-            slots = max(slots, n_woven)
-            done = 0
-            for j in range(slots):
-                pf = weave(c_quant, j) if j < n_woven else None
-                ps = pool_nodes(c_pool, j) if j < n_pairs else None
-                upto = min(len(s_planes), -(-len(s_planes) * (j + 1) // slots))
-                for plane in s_planes[done:upto]:
-                    widen(c_wide, plane)
-                done = upto
-                if j < n_woven:
-                    empty_woven(c_quant, j, pf)
-                if turned:
-                    empty_rows(c_quant, *turned[0])
-                    turned = turned[1:]
-                if j < n_pairs:
-                    empty_sums(c_pool, j, ps)
-            for item in turned:
-                empty_rows(c_quant, *item)
-            if has_pool:
-                quantize_m(c_pool)
-            outs = []
-            if has_out:
-                quantize_a(c_out)
-                outs = [(b,) + project(c_out, b) for b in range((CHUNKS[c_out] + 511) // 512)]
-            if has_quant:
-                quantize_h(c_quant, 0)
-            if has_quant:
-                quantize_h(c_quant, 1)
             if step == 0:
-                make_stationary()
-            for plane in v_planes:
-                widen(c_wide, plane)
-            for item in outs:
-                add_bias(c_out, *item)
-            if has_out:
-                relu(c_out)
-                store(c_out)
+                quantize_nodes()
+            if step == 1:
+                spread_bias()
+            if 0 <= to_finish < n_chunks:
+                quantize_rows(to_finish)
+                quantize_sums(to_finish)
+            if 0 <= to_quantize < n_chunks:
+                for g in range(GROUPS):
+                    interleave(to_quantize, g)
+                for g in range(GROUPS):
+                    quantize_events(to_quantize, g)
+            if 0 <= to_pool < n_chunks:
+                for j in range(CHUNKS[to_pool] // PAIR):
+                    empty_sums(to_pool, j, pool_nodes(to_pool, j))
+            if 0 <= to_finish < n_chunks:
+                if to_finish < FIRST_DIRECT:
+                    finish_turned(to_finish)
+                else:
+                    finish_direct(to_finish)
+                store(to_finish)
+            if to_widen < n_chunks:
+                for plane in range(PLANES):
+                    widen(to_widen, plane)
+            if 0 <= to_quantize < n_chunks:
+                for b in range((CHUNKS[to_quantize] + 2 * PAIR - 1) // (2 * PAIR)):
+                    turn_rows(to_quantize, b)

from contextlib import ExitStack

import concourse.mybir as mybir
from concourse.masks import make_identity

F32 = mybir.dt.float32
BF16 = mybir.dt.bfloat16
U32 = mybir.dt.uint32
I32 = mybir.dt.int32
U8 = mybir.dt.uint8
FP8 = mybir.dt.float8_e4m3fn
FP8X4 = mybir.dt.float8_e4m3fn_x4
FP4X4 = mybir.dt.float4_e2m1fn_x4
ALU = mybir.AluOpType
COPY = mybir.ActivationFunctionType.Copy
RELU = mybir.ActivationFunctionType.Relu

NODES, EVENTS, HIDDEN, OUT = 1024, 8192, 256, 128

P = 128
PACK = 4
PASS = P * PACK
GROUPS = NODES // PASS
PAIR = 2 * P
QUADS = HIDDEN // PACK
BANK = 512
PLANES = GROUPS * PACK

CHUNKS = (256, 512, 1024, 1024, 1024, 1024, 1024, 1024, 512, 512, 256)
VECTOR_PLANES = (5, 2, 3, 3, 4, 4, 4, 3, 1, 4, 0)
FIRST_DIRECT = 7
AHEAD = 4

FLOPS = 2 * NODES * EVENTS * HIDDEN + 2 * EVENTS * 2 * HIDDEN * OUT


def tile_mymodel_icdm_pa_t_w4_kernel(
    tc, H_A_bytes, H_A_scale, H_mean_A, H_mean_M, wEA1_words, wEA1_scales, bEA1, out
):
    nc = tc.nc
    n_chunks = len(CHUNKS)
    first_event = [sum(CHUNKS[:c]) for c in range(n_chunks)]

    with ExitStack() as ctx:
        keep = ctx.enter_context(tc.tile_pool(name="keep", bufs=1))
        work = ctx.enter_context(tc.tile_pool(name="work", bufs=2))
        psum = ctx.enter_context(tc.psum_pool(name="psum", bufs=2))
        ctx.enter_context(tc.manual_schedule(engines={mybir.EngineType.SP}))

        warm = keep.tile([P, 1], F32, name="warm")
        nc.vector.memset(warm[:], 0.0)
        nc.scalar.activation(out=warm[:], in_=warm[:], func=COPY)


        n_blocks = 2 * PLANES + 1
        node_codes = keep.tile([P, n_blocks * QUADS], U32, name="node_codes", align_bytes=64)
        node_scales = keep.tile([P, n_blocks * QUADS], U8, name="node_scales", align_bytes=64)
        nc.vector.memset(node_codes[:], 0)
        nc.vector.memset(node_scales[:].bitcast(I32), 0)

        weight = keep.tile([P, 4, 2 * OUT], U8, name="weight", align_bytes=64)
        weight_scales = keep.tile([P, 4, OUT], U8, name="weight_scales", align_bytes=64)
        nc.vector.memset(weight[:].rearrange("p v b -> p (v b)").bitcast(I32), 0)
        nc.vector.memset(weight_scales[:].rearrange("p v n -> p (v n)").bitcast(I32), 0)

        bias_in = keep.tile([P, 1], BF16, name="bias_in")
        bias_column = keep.tile([P, 1], F32, name="bias_column")
        bias_row = keep.tile([P, OUT], BF16, name="bias_row")
        bias_spread = keep.tile([P, BANK // OUT, OUT], F32, name="bias_spread")
        ones = keep.tile([P, P], BF16, name="ones")
        nc.vector.memset(bias_row[:], 0.0)
        nc.vector.memset(ones[:], 1.0)
        identity = keep.tile([P, P], F32, name="identity")
        make_identity(nc, identity[:])


        plane_scales = keep.tile([P, GROUPS, PACK], F32, name="plane_scales")
        nc.sync.dma_start(out=plane_scales[:], in_=H_A_scale.rearrange("(g p t) o -> p g (t o)", p=P, t=PACK))

        event_bytes = {}
        event_rows = {}

        def load_bytes(c):
            events = slice(first_event[c], first_event[c] + CHUNKS[c])
            for g in range(GROUPS):
                raw = keep.tile([P, PACK, CHUNKS[c]], U8, name="bytes_%d_%d" % (c, g), align_bytes=64)
                event_bytes[c, g] = raw
                nodes = slice(PASS * g, PASS * (g + 1))
                nc.sync.dma_start(out=raw[:], in_=H_A_bytes[nodes, events].rearrange("(p t) e -> p t e", t=PACK))

        def load_rows(c):
            events = slice(first_event[c], first_event[c] + CHUNKS[c])
            rows = keep.tile([P, CHUNKS[c] // P, HIDDEN], BF16, name="rows_%d" % c, align_bytes=64)
            event_rows[c] = rows
            nc.sync.dma_start(out=rows[:], in_=H_mean_M[events, :].rearrange("(r i) k -> i r k", i=P))

        load_bytes(0)
        load_bytes(1)
        nc.sync.dma_start(out=bias_in[:], in_=bEA1.rearrange("(c o) -> c o", o=1))
        nc.sync.dma_start(out=bias_row[0:1, :], in_=bEA1.rearrange("(o c) -> o c", o=1))
        node_rows = keep.tile([P, GROUPS, PACK, HIDDEN], BF16, name="node_rows", align_bytes=64)
        for g in range(GROUPS):
            nodes = slice(PASS * g, PASS * (g + 1))
            nc.sync.dma_start(out=node_rows[:, g], in_=H_mean_A[nodes, :].rearrange("(p j) c -> p j c", j=PACK))
        load_rows(0)
        load_bytes(2)
        load_rows(1)
        load_bytes(3)
        load_rows(2)
        word_halves = wEA1_words[0].rearrange("(h p) b -> p h b", h=2).bitcast(I32)
        scale_quadrants = wEA1_scales[0].rearrange("(h r b) n -> r b h n", h=2, r=2)
        for side in range(2):
            forms = slice(2 * side, 2 * side + 2)
            nc.sync.dma_start(out=weight[QUADS * side : QUADS * (side + 1), forms, :].bitcast(I32), in_=word_halves)
        for quadrant in range(4):
            side, r = divmod(quadrant, 2)
            forms = slice(2 * side, 2 * side + 2)
            nc.sync.dma_start(
                out=weight_scales[32 * quadrant : 32 * quadrant + 4, forms, :].bitcast(I32),
                in_=scale_quadrants[r].bitcast(I32),
            )
        load_rows(3)


        def spread_bias():
            po = psum.tile([P, BANK // OUT, OUT], F32, name="po", bufs=2)
            for i in range(BANK // OUT):
                nc.tensor.matmul(out=po[:, i, :], lhsT=ones[:], rhs=bias_row[:], start=True, stop=True)
            nc.scalar.copy(out=bias_spread[:], in_=po[:])
            nc.scalar.copy(out=bias_column[:], in_=bias_in[:])

        def quantize_nodes():
            grouped = keep.tile([P, GROUPS, PACK, QUADS, PACK], BF16, name="node_grouped", align_bytes=64)
            for g in range(GROUPS):
                nc.vector.tensor_copy(out=grouped[:, g], in_=node_rows[:, g].rearrange("p j (q t) -> p t q j", t=PACK))
            for g in range(GROUPS):
                for t in range(PACK):
                    c0 = (2 * (PACK * g + t) + 1) * QUADS
                    nc.vector.quantize_mx(
                        out=node_codes[:, c0 : c0 + QUADS].bitcast(FP8X4),
                        scales=node_scales[:, c0 : c0 + QUADS],
                        in_=grouped[:, g, t].rearrange("p q j -> p (q j)"),
                    )


        wide, h_grouped, h_codes, h_scales = {}, {}, {}, {}
        m_grouped, m_codes, m_scales = {}, {}, {}
        a_grouped, a_codes, a_scales = {}, {}, {}
        results = {}

        def widen(c, plane):
            g, t = divmod(plane, PACK)
            if t == 0:
                planes = work.tile([P, PACK, CHUNKS[c]], BF16, name="wide", bufs=4, align_bytes=64)
                wide[c, g] = planes
            values = event_bytes[c, g][:, t, :].bitcast(FP8)
            scale = plane_scales[:, g, t : t + 1]
            if plane < PLANES - VECTOR_PLANES[c]:
                nc.scalar.activation(out=wide[c, g][:, t, :], in_=values, func=COPY, scale=scale)
            else:
                nc.vector.tensor_scalar(
                    out=wide[c, g][:, t, :], in0=values, scalar1=scale, scalar2=None, op0=ALU.mult
                )

        def interleave(c, g):
            grouped = work.tile([P, PACK * CHUNKS[c]], BF16, name="h_grouped", bufs=3, align_bytes=64)
            h_grouped[c, g] = grouped
            nc.vector.tensor_copy(
                out=grouped[:].rearrange("p (e i t) -> p e t i", i=4, t=PACK),
                in_=wide[c, g][:].rearrange("p t (e i) -> p e t i", i=4),
            )

        def quantize_events(c, g):
            if g == 0:
                codes = work.tile([P, GROUPS, CHUNKS[c]], U32, name="h_codes", bufs=2, align_bytes=64)
                scales = work.tile([P, GROUPS, CHUNKS[c]], U8, name="h_scales", bufs=2, align_bytes=64)
                h_codes[c], h_scales[c] = codes, scales
            nc.vector.quantize_mx(
                out=h_codes[c][:, g, :].bitcast(FP8X4), scales=h_scales[c][:, g, :], in_=h_grouped[c, g][:]
            )

        def pool_nodes(c, j):
            ps = psum.tile([P, PACK, P], F32, name="ps", bufs=2)
            for t in range(PACK):
                for side in range(2):
                    cols = slice(PAIR * j + P * side, PAIR * j + P * (side + 1))
                    for g in range(GROUPS):
                        c0 = (2 * (PACK * g + t) + 1 - side) * QUADS
                        nc.tensor.matmul_mx(
                            out=ps[:, t, :],
                            lhsT=node_codes[:, c0 : c0 + P].bitcast(FP8X4),
                            lhsT_scale=node_scales[:, c0 : c0 + P],
                            rhs=h_codes[c][:, g, cols].bitcast(FP8X4),
                            rhs_scale=h_scales[c][:, g, cols],
                            start=(side == 0 and g == 0),
                            stop=(side == 1 and g == GROUPS - 1),
                        )
            return ps

        def empty_sums(c, j, ps):
            if j == 0:
                grouped = work.tile([P, PACK * CHUNKS[c] // 2], BF16, name="a_grouped", bufs=2, align_bytes=64)
                a_grouped[c] = grouped
            nc.scalar.copy(
                out=a_grouped[c][:, BANK * j : BANK * (j + 1)].rearrange("p (n t) -> p n t", t=PACK),
                in_=ps[:].rearrange("p t n -> p n t"),
            )

        def turn_rows(c, b):
            n_pairs = min(2, CHUNKS[c] // PAIR - 2 * b)
            if b == 0:
                grouped = work.tile([P, PACK * CHUNKS[c] // 2], BF16, name="m_grouped", bufs=2, align_bytes=64)
                m_grouped[c] = grouped
            words = event_rows[c][:].rearrange("p r k -> p (r k)").bitcast(F32)
            pt = psum.tile([P, n_pairs, 2, P], F32, name="pt", bufs=2)
            for j in range(n_pairs):
                w0 = HIDDEN * (2 * b + j)
                for u in range(2):
                    nc.tensor.transpose(pt[:, j, u, :], words[:, w0 + u : w0 + HIDDEN : 2], identity[:])
            nc.scalar.copy(
                out=m_grouped[c][:]
                .bitcast(F32)[:, BANK * b : BANK * b + HIDDEN * n_pairs]
                .rearrange("p (j n u) -> p j n u", n=P, u=2),
                in_=pt[:].rearrange("p j u n -> p j n u"),
            )

        def quantize_rows(c):
            codes = work.tile([P, CHUNKS[c] // 2], U32, name="m_codes", bufs=3, align_bytes=64)
            scales = work.tile([P, CHUNKS[c] // 2], U8, name="m_scales", bufs=3, align_bytes=64)
            m_codes[c], m_scales[c] = codes, scales
            nc.vector.quantize_mx(out=codes[:].bitcast(FP8X4), scales=scales[:], in_=m_grouped[c][:])

        def quantize_sums(c):
            codes = work.tile([P, CHUNKS[c] // 2], U32, name="a_codes", bufs=2, align_bytes=64)
            scales = work.tile([P, CHUNKS[c] // 2], U8, name="a_scales", bufs=2, align_bytes=64)
            a_codes[c], a_scales[c] = codes, scales
            nc.vector.quantize_mx(out=codes[:].bitcast(FP8X4), scales=scales[:], in_=a_grouped[c][:])

        def halves(c):
            return ((0, m_codes[c], m_scales[c]), (1, a_codes[c], a_scales[c]))

        def new_result(c):
            result = work.tile([P, CHUNKS[c] // P, OUT], F32, name="result", bufs=3)
            results[c] = result

        def finish_direct(c):
            new_result(c)
            n_sets = CHUNKS[c] // P
            for r0 in range(0, n_sets, BANK // OUT):
                n = min(BANK // OUT, n_sets - r0)
                po = psum.tile([P, n, OUT], F32, name="po", bufs=2)
                for i in range(n):
                    pair, side = divmod(r0 + i, 2)
                    cols = slice(P * pair, P * (pair + 1))
                    for half, codes, scales in halves(c):
                        nc.tensor.matmul_mx(
                            out=po[:, i, :],
                            lhsT=codes[:, cols].bitcast(FP8X4),
                            lhsT_scale=scales[:, cols],
                            rhs=weight[:, 2 * side + half, :].bitcast(FP4X4),
                            rhs_scale=weight_scales[:, 2 * side + half, :],
                            start=(half == 0),
                            stop=(half == 1),
                        )
                nc.vector.tensor_tensor(
                    out=results[c][:, r0 : r0 + n, :], in0=po[:], in1=bias_spread[:, 0:n, :], op=ALU.add
                )
            nc.vector.tensor_scalar(out=results[c][:], in0=results[c][:], scalar1=0.0, scalar2=None, op0=ALU.max)

        def finish_turned(c):
            n = CHUNKS[c] // 2
            width = BANK if n == BANK else P
            turned = []
            for side in range(2):
                po = psum.tile([P, n], F32, name="po", bufs=2)
                for c0 in range(0, n, width):
                    cols = slice(c0, c0 + width)
                    for half, codes, scales in halves(c):
                        nc.tensor.matmul_mx(
                            out=po[:, cols],
                            lhsT=weight[:, 2 * side + half, :].bitcast(FP4X4),
                            lhsT_scale=weight_scales[:, 2 * side + half, :],
                            rhs=codes[:, cols].bitcast(FP8X4),
                            rhs_scale=scales[:, cols],
                            start=(half == 0),
                            stop=(half == 1),
                        )
                channels = work.tile([P, n], F32, name="channels", bufs=2)
                nc.scalar.activation(out=channels[:], in_=po[:], func=RELU, bias=bias_column[:])
                turned.append(channels)
            new_result(c)
            for side in range(2):
                pz = psum.tile([P, n // P, OUT], F32, name="pz", bufs=2)
                for j in range(n // P):
                    nc.tensor.transpose(pz[:, j, :], turned[side][:, P * j : P * (j + 1)], identity[:])
                nc.scalar.copy(out=results[c][:, side::2, :], in_=pz[:])

        def store(c):
            events = slice(first_event[c], first_event[c] + CHUNKS[c])
            nc.sync.dma_start(out=out[events, :].rearrange("(r i) k -> i r k", i=P), in_=results[c][:])


        for step in range(-1, n_chunks + 2):
            to_widen, to_quantize, to_pool, to_finish = step + 1, step, step - 1, step - 2
            if 0 <= step < n_chunks - AHEAD:
                load_bytes(step + AHEAD)
                load_rows(step + AHEAD)
            if step == 0:
                quantize_nodes()
            if step == 1:
                spread_bias()
            if 0 <= to_finish < n_chunks:
                quantize_rows(to_finish)
                quantize_sums(to_finish)
            if 0 <= to_quantize < n_chunks:
                for g in range(GROUPS):
                    interleave(to_quantize, g)
                for g in range(GROUPS):
                    quantize_events(to_quantize, g)
            if 0 <= to_pool < n_chunks:
                for j in range(CHUNKS[to_pool] // PAIR):
                    empty_sums(to_pool, j, pool_nodes(to_pool, j))
            if 0 <= to_finish < n_chunks:
                if to_finish < FIRST_DIRECT:
                    finish_turned(to_finish)
                else:
                    finish_direct(to_finish)
                store(to_finish)
            if to_widen < n_chunks:
                for plane in range(PLANES):
                    widen(to_widen, plane)
            if 0 <= to_quantize < n_chunks:
                for b in range((CHUNKS[to_quantize] + 2 * PAIR - 1) // (2 * PAIR)):
                    turn_rows(to_quantize, b)
